import numpy as np
import ml_dtypes

BF16 = ml_dtypes.bfloat16


def bf(x):
    return np.asarray(x, np.float32).astype(BF16)


def f32(x):
    return np.asarray(x, np.float32)


def f64(x):
    return np.asarray(x).astype(np.float64)


def striped(idx):
    return np.tile(idx.reshape(-1, 16).T, (8, 1))


D, S, N = 128, 1024, 512


def setup_inputs():
    return {"table": bf(np.random.standard_normal((D, S))), "wq": bf(2.0 * np.random.standard_normal((D, D)) / np.sqrt(D)), "wk": bf(np.random.standard_normal((D, D)) / np.sqrt(D)), "offs": striped(np.random.permutation(S)[:N])}


def reference(table, wq, wk, offs):
    idx = offs[:16].T.reshape(-1)
    q = f64(wq).T @ f64(table)[:, idx]
    k = f64(wk).T @ f64(table)
    return k.T @ q / np.sqrt(D)

@@ -1,0 +1,56 @@
+import math
+
+import concourse.mybir as mybir
+
+D = 128
+S = 1024
+N = 512
+P = 128
+BANK = 512
+
+BF16, F32, U16 = mybir.dt.bfloat16, mybir.dt.float32, mybir.dt.uint16
+COPY = mybir.ActivationFunctionType.Copy
+
+FLOPS = 2 * D * D * N + 2 * D * D * S + 2 * D * S * N
+
+
+def tile_informermodel_kernel(tc, table, wq, wk, offs, out):
+    nc = tc.nc
+    inv_sqrt_d = 1.0 / math.sqrt(D)
+
+    with (
+        tc.tile_pool(name="held", bufs=1) as held,
+        tc.tile_pool(name="staging", bufs=4) as staging,
+        tc.psum_pool(name="psum", bufs=8) as psum,
+    ):
+        offsets = held.tile([P, N // 16], U16, name="offsets")
+        nc.sync.dma_start(offsets[:], offs)
+        table_sb = held.tile([D, S], BF16, name="table_sb")
+        nc.sync.dma_start(table_sb[:], table)
+        wq_sb = held.tile([D, D], BF16, name="wq_sb")
+        nc.scalar.dma_start(wq_sb[:], wq)
+        wk_sb = held.tile([D, D], BF16, name="wk_sb")
+        nc.scalar.dma_start(wk_sb[:], wk)
+
+        q_ps = psum.tile([D, N], F32, name="bank")
+        nc.tensor.matmul(q_ps[:], wq_sb[:], table_sb[:].indirect(offsets[:]), start=True, stop=True)
+        q_bf = held.tile([D, N], BF16, name="q_bf")
+        nc.vector.tensor_copy(q_bf[:], q_ps[:])
+
+        k_bf = held.tile([D, S], BF16, name="k_bf")
+        for c in range(S // BANK):
+            cols = slice(c * BANK, (c + 1) * BANK)
+            k_ps = psum.tile([D, BANK], F32, name="bank")
+            nc.tensor.matmul(k_ps[:], wk_sb[:], table_sb[:, cols], start=True, stop=True)
+            nc.scalar.copy(k_bf[:, cols], k_ps[:])
+
+        for b in range(S // P):
+            rows = slice(b * P, (b + 1) * P)
+            s_ps = psum.tile([P, N], F32, name="bank")
+            nc.tensor.matmul(s_ps[:], k_bf[:, rows], q_bf[:], start=True, stop=True)
+            scores = staging.tile([P, N], F32, name="scores")
+            if b % 2 == 0:
+                nc.vector.tensor_scalar_mul(scores[:], s_ps[:], inv_sqrt_d)
+            else:
+                nc.scalar.activation(scores[:], s_ps[:], COPY, scale=inv_sqrt_d)
+            nc.sync.dma_start(out[rows, :], scores[:])

@@ -7,6 +7,7 @@ S = 1024
 N = 512
 P = 128
 BANK = 512
+HALF = N // 2
 
 BF16, F32, U16 = mybir.dt.bfloat16, mybir.dt.float32, mybir.dt.uint16
 COPY = mybir.ActivationFunctionType.Copy
@@ -20,37 +21,47 @@ def tile_informermodel_kernel(tc, table, wq, wk, offs, out):
 
     with (
         tc.tile_pool(name="held", bufs=1) as held,
-        tc.tile_pool(name="staging", bufs=4) as staging,
-        tc.psum_pool(name="psum", bufs=8) as psum,
+        tc.psum_pool(name="psum", bufs=4) as psum,
     ):
-        offsets = held.tile([P, N // 16], U16, name="offsets")
-        nc.sync.dma_start(offsets[:], offs)
         table_sb = held.tile([D, S], BF16, name="table_sb")
         nc.sync.dma_start(table_sb[:], table)
-        wq_sb = held.tile([D, D], BF16, name="wq_sb")
-        nc.scalar.dma_start(wq_sb[:], wq)
         wk_sb = held.tile([D, D], BF16, name="wk_sb")
-        nc.scalar.dma_start(wk_sb[:], wk)
-
-        q_ps = psum.tile([D, N], F32, name="bank")
-        nc.tensor.matmul(q_ps[:], wq_sb[:], table_sb[:].indirect(offsets[:]), start=True, stop=True)
-        q_bf = held.tile([D, N], BF16, name="q_bf")
-        nc.vector.tensor_copy(q_bf[:], q_ps[:])
+        nc.sync.dma_start(wk_sb[:], wk)
+        offsets = held.tile([P, N // 16], U16, name="offsets")
+        nc.sync.dma_start(offsets[:], offs)
+        wq_sb = held.tile([D, D], BF16, name="wq_sb")
+        nc.sync.dma_start(wq_sb[:], wq)
 
         k_bf = held.tile([D, S], BF16, name="k_bf")
-        for c in range(S // BANK):
-            cols = slice(c * BANK, (c + 1) * BANK)
-            k_ps = psum.tile([D, BANK], F32, name="bank")
-            nc.tensor.matmul(k_ps[:], wk_sb[:], table_sb[:, cols], start=True, stop=True)
-            nc.scalar.copy(k_bf[:, cols], k_ps[:])
+        q_left = held.tile([D, HALF], BF16, name="q_left")
+        q_right = held.tile([D, HALF], BF16, name="q_right")
+
+        k_ps0 = psum.tile([D, BANK], BF16, name="k_ps0", tag="left")
+        nc.tensor.matmul(k_ps0[:], wk_sb[:], table_sb[:, 0:BANK], start=True, stop=True)
+        nc.vector.tensor_copy(k_bf[:, 0:BANK], k_ps0[:])
+
+        q_ps_left = psum.tile([D, HALF], F32, name="q_ps_left", tag="left")
+        nc.tensor.matmul(
+            q_ps_left[:], wq_sb[:], table_sb[:].indirect(offsets[:, 0 : HALF // 16]), start=True, stop=True
+        )
+        nc.vector.tensor_copy(q_left[:], q_ps_left[:])
+        q_ps_right = psum.tile([D, HALF], F32, name="q_ps_right", tag="right")
+        nc.tensor.matmul(
+            q_ps_right[:], wq_sb[:], table_sb[:].indirect(offsets[:, HALF // 16 : N // 16]), start=True, stop=True
+        )
+        nc.scalar.activation(q_right[:], q_ps_right[:], COPY)
+
+        k_ps1 = psum.tile([D, BANK], BF16, name="k_ps1", tag="right")
+        nc.tensor.matmul(k_ps1[:], wk_sb[:], table_sb[:, BANK:S], start=True, stop=True)
+        nc.scalar.activation(k_bf[:, BANK:S], k_ps1[:], COPY)
 
         for b in range(S // P):
             rows = slice(b * P, (b + 1) * P)
-            s_ps = psum.tile([P, N], F32, name="bank")
-            nc.tensor.matmul(s_ps[:], k_bf[:, rows], q_bf[:], start=True, stop=True)
-            scores = staging.tile([P, N], F32, name="scores")
-            if b % 2 == 0:
-                nc.vector.tensor_scalar_mul(scores[:], s_ps[:], inv_sqrt_d)
-            else:
-                nc.scalar.activation(scores[:], s_ps[:], COPY, scale=inv_sqrt_d)
+            scores = held.tile([P, N], F32, name=f"scores{b}")
+            s_ps_left = psum.tile([P, HALF], F32, name="s_ps_left", tag="left")
+            nc.tensor.matmul(s_ps_left[:], k_bf[:, rows], q_left[:], start=True, stop=True)
+            nc.vector.tensor_scalar_mul(scores[:, 0:HALF], s_ps_left[:], inv_sqrt_d)
+            s_ps_right = psum.tile([P, HALF], F32, name="s_ps_right", tag="right")
+            nc.tensor.matmul(s_ps_right[:], k_bf[:, rows], q_right[:], start=True, stop=True)
+            nc.scalar.activation(scores[:, HALF:N], s_ps_right[:], COPY, scale=inv_sqrt_d)
             nc.sync.dma_start(out[rows, :], scores[:])

@@ -7,6 +7,7 @@ S = 1024
 N = 512
 P = 128
 BANK = 512
+WARM_UP = 4
 HALF = N // 2
 
 BF16, F32, U16 = mybir.dt.bfloat16, mybir.dt.float32, mybir.dt.uint16
@@ -31,6 +32,12 @@ def tile_informermodel_kernel(tc, table, wq, wk, offs, out):
         nc.sync.dma_start(offsets[:], offs)
         wq_sb = held.tile([D, D], BF16, name="wq_sb")
         nc.sync.dma_start(wq_sb[:], wq)
+
+        zeros = held.tile([P, BANK], BF16, name="zeros")
+        nc.vector.memset(zeros[:], 0.0)
+        warm_ps = psum.tile([P, BANK], F32, name="warm_ps", tag="left")
+        for _ in range(WARM_UP):
+            nc.tensor.matmul(warm_ps[:], zeros[:, 0:P], zeros[:], start=True, stop=True)
 
         k_bf = held.tile([D, S], BF16, name="k_bf")
         q_left = held.tile([D, HALF], BF16, name="q_left")

@@ -9,6 +9,7 @@ P = 128
 BANK = 512
 WARM_UP = 4
 HALF = N // 2
+R = BANK // P
 
 BF16, F32, U16 = mybir.dt.bfloat16, mybir.dt.float32, mybir.dt.uint16
 COPY = mybir.ActivationFunctionType.Copy
@@ -16,9 +17,21 @@ COPY = mybir.ActivationFunctionType.Copy
 FLOPS = 2 * D * D * N + 2 * D * D * S + 2 * D * S * N
 
 
+def doubling_groups(blocks):
+    groups = []
+    first = 0
+    while first < blocks:
+        width = max(first, 1)
+        groups.append((first, first + width))
+        first += width
+    return groups
+
+
 def tile_informermodel_kernel(tc, table, wq, wk, offs, out):
     nc = tc.nc
     inv_sqrt_d = 1.0 / math.sqrt(D)
+
+    out_blocks = out.rearrange("(c p r) j -> c p r j", p=P, r=R)
 
     with (
         tc.tile_pool(name="held", bufs=1) as held,
@@ -39,13 +52,13 @@ def tile_informermodel_kernel(tc, table, wq, wk, offs, out):
         for _ in range(WARM_UP):
             nc.tensor.matmul(warm_ps[:], zeros[:, 0:P], zeros[:], start=True, stop=True)
 
-        k_bf = held.tile([D, S], BF16, name="k_bf")
         q_left = held.tile([D, HALF], BF16, name="q_left")
         q_right = held.tile([D, HALF], BF16, name="q_right")
+        k_blocks = held.tile([D, S // BANK, R, P], BF16, name="k_blocks")
 
         k_ps0 = psum.tile([D, BANK], BF16, name="k_ps0", tag="left")
         nc.tensor.matmul(k_ps0[:], wk_sb[:], table_sb[:, 0:BANK], start=True, stop=True)
-        nc.vector.tensor_copy(k_bf[:, 0:BANK], k_ps0[:])
+        nc.vector.tensor_copy(k_blocks[:, 0, :, :], k_ps0[:].rearrange("m (p r) -> m r p", r=R))
 
         q_ps_left = psum.tile([D, HALF], F32, name="q_ps_left", tag="left")
         nc.tensor.matmul(
@@ -60,15 +73,18 @@ def tile_informermodel_kernel(tc, table, wq, wk, offs, out):
 
         k_ps1 = psum.tile([D, BANK], BF16, name="k_ps1", tag="right")
         nc.tensor.matmul(k_ps1[:], wk_sb[:], table_sb[:, BANK:S], start=True, stop=True)
-        nc.scalar.activation(k_bf[:, BANK:S], k_ps1[:], COPY)
+        nc.scalar.activation(k_blocks[:, 1, :, :], k_ps1[:].rearrange("m (p r) -> m r p", r=R), COPY)
 
-        for b in range(S // P):
-            rows = slice(b * P, (b + 1) * P)
-            scores = held.tile([P, N], F32, name=f"scores{b}")
-            s_ps_left = psum.tile([P, HALF], F32, name="s_ps_left", tag="left")
-            nc.tensor.matmul(s_ps_left[:], k_bf[:, rows], q_left[:], start=True, stop=True)
-            nc.vector.tensor_scalar_mul(scores[:, 0:HALF], s_ps_left[:], inv_sqrt_d)
-            s_ps_right = psum.tile([P, HALF], F32, name="s_ps_right", tag="right")
-            nc.tensor.matmul(s_ps_right[:], k_bf[:, rows], q_right[:], start=True, stop=True)
-            nc.scalar.activation(scores[:, HALF:N], s_ps_right[:], COPY, scale=inv_sqrt_d)
-            nc.sync.dma_start(out[rows, :], scores[:])
+        scores = [held.tile([P, R, N], F32, name=f"scores{c}") for c in range(S // BANK)]
+        for first, end in doubling_groups(S // P):
+            c = first // R
+            assert end <= (c + 1) * R, "a store stays inside one half of the time steps"
+            for r in range(first - c * R, end - c * R):
+                s_ps_left = psum.tile([P, HALF], F32, name="s_ps_left", tag="left")
+                nc.tensor.matmul(s_ps_left[:], k_blocks[:, c, r, :], q_left[:], start=True, stop=True)
+                nc.vector.tensor_scalar_mul(scores[c][:, r, 0:HALF], s_ps_left[:], inv_sqrt_d)
+                s_ps_right = psum.tile([P, HALF], F32, name="s_ps_right", tag="right")
+                nc.tensor.matmul(s_ps_right[:], k_blocks[:, c, r, :], q_right[:], start=True, stop=True)
+                nc.scalar.activation(scores[c][:, r, HALF:N], s_ps_right[:], COPY, scale=inv_sqrt_d)
+            stored = slice(first - c * R, end - c * R)
+            nc.sync.dma_start(out_blocks[c, :, stored, :], scores[c][:, stored, :])

@@ -9,7 +9,6 @@ P = 128
 BANK = 512
 WARM_UP = 4
 HALF = N // 2
-R = BANK // P
 
 BF16, F32, U16 = mybir.dt.bfloat16, mybir.dt.float32, mybir.dt.uint16
 COPY = mybir.ActivationFunctionType.Copy
@@ -31,7 +30,7 @@ def tile_informermodel_kernel(tc, table, wq, wk, offs, out):
     nc = tc.nc
     inv_sqrt_d = 1.0 / math.sqrt(D)
 
-    out_blocks = out.rearrange("(c p r) j -> c p r j", p=P, r=R)
+    groups = doubling_groups(S // P)
 
     with (
         tc.tile_pool(name="held", bufs=1) as held,
@@ -54,37 +53,44 @@ def tile_informermodel_kernel(tc, table, wq, wk, offs, out):
 
         q_left = held.tile([D, HALF], BF16, name="q_left")
         q_right = held.tile([D, HALF], BF16, name="q_right")
-        k_blocks = held.tile([D, S // BANK, R, P], BF16, name="k_blocks")
+        k_sb = held.tile([D, S], BF16, name="k_sb")
 
-        k_ps0 = psum.tile([D, BANK], BF16, name="k_ps0", tag="left")
-        nc.tensor.matmul(k_ps0[:], wk_sb[:], table_sb[:, 0:BANK], start=True, stop=True)
-        nc.vector.tensor_copy(k_blocks[:, 0, :, :], k_ps0[:].rearrange("m (p r) -> m r p", r=R))
+        def project_keys(g):
+            first, end = groups[g]
+            steps = slice(first * P, end * P)
+            if g % 2 == 0:
+                k_ps = psum.tile([D, (end - first) * P], BF16, name="k_ps_right", tag="right")
+                nc.tensor.matmul(k_ps[:], wk_sb[:], table_sb[:, steps], start=True, stop=True)
+                nc.scalar.activation(k_sb[:, steps], k_ps[:], COPY)
+            else:
+                k_ps = psum.tile([D, (end - first) * P], BF16, name="k_ps_left", tag="left")
+                nc.tensor.matmul(k_ps[:], wk_sb[:], table_sb[:, steps], start=True, stop=True)
+                nc.vector.tensor_copy(k_sb[:, steps], k_ps[:])
 
         q_ps_left = psum.tile([D, HALF], F32, name="q_ps_left", tag="left")
         nc.tensor.matmul(
             q_ps_left[:], wq_sb[:], table_sb[:].indirect(offsets[:, 0 : HALF // 16]), start=True, stop=True
         )
         nc.vector.tensor_copy(q_left[:], q_ps_left[:])
+        project_keys(0)
         q_ps_right = psum.tile([D, HALF], F32, name="q_ps_right", tag="right")
         nc.tensor.matmul(
             q_ps_right[:], wq_sb[:], table_sb[:].indirect(offsets[:, HALF // 16 : N // 16]), start=True, stop=True
         )
         nc.scalar.activation(q_right[:], q_ps_right[:], COPY)
 
-        k_ps1 = psum.tile([D, BANK], BF16, name="k_ps1", tag="right")
-        nc.tensor.matmul(k_ps1[:], wk_sb[:], table_sb[:, BANK:S], start=True, stop=True)
-        nc.scalar.activation(k_blocks[:, 1, :, :], k_ps1[:].rearrange("m (p r) -> m r p", r=R), COPY)
-
-        scores = [held.tile([P, R, N], F32, name=f"scores{c}") for c in range(S // BANK)]
-        for first, end in doubling_groups(S // P):
-            c = first // R
-            assert end <= (c + 1) * R, "a store stays inside one half of the time steps"
-            for r in range(first - c * R, end - c * R):
+        for g, (first, end) in enumerate(groups):
+            if g + 1 < len(groups):
+                project_keys(g + 1)
+            width = end - first
+            steps = slice(first * P, end * P)
+            k_blocks = k_sb[:, steps].rearrange("m (p r) -> m r p", r=width)
+            scores = held.tile([P, width, N], F32, name=f"scores{g}")
+            for r in range(width):
                 s_ps_left = psum.tile([P, HALF], F32, name="s_ps_left", tag="left")
-                nc.tensor.matmul(s_ps_left[:], k_blocks[:, c, r, :], q_left[:], start=True, stop=True)
-                nc.vector.tensor_scalar_mul(scores[c][:, r, 0:HALF], s_ps_left[:], inv_sqrt_d)
+                nc.tensor.matmul(s_ps_left[:], k_blocks[:, r, :], q_left[:], start=True, stop=True)
+                nc.vector.tensor_scalar_mul(scores[:, r, 0:HALF], s_ps_left[:], inv_sqrt_d)
                 s_ps_right = psum.tile([P, HALF], F32, name="s_ps_right", tag="right")
-                nc.tensor.matmul(s_ps_right[:], k_blocks[:, c, r, :], q_right[:], start=True, stop=True)
-                nc.scalar.activation(scores[c][:, r, HALF:N], s_ps_right[:], COPY, scale=inv_sqrt_d)
-            stored = slice(first - c * R, end - c * R)
-            nc.sync.dma_start(out_blocks[c, :, stored, :], scores[c][:, stored, :])
+                nc.tensor.matmul(s_ps_right[:], k_blocks[:, r, :], q_right[:], start=True, stop=True)
+                nc.scalar.activation(scores[:, r, HALF:N], s_ps_right[:], COPY, scale=inv_sqrt_d)
+            nc.sync.dma_start(out[steps, :].rearrange("(p r) j -> p r j", r=width), scores[:])

@@ -8,7 +8,7 @@ N = 512
 P = 128
 BANK = 512
 WARM_UP = 4
-HALF = N // 2
+LOOK_UP = 128
 
 BF16, F32, U16 = mybir.dt.bfloat16, mybir.dt.float32, mybir.dt.uint16
 COPY = mybir.ActivationFunctionType.Copy
@@ -47,37 +47,48 @@ def tile_informermodel_kernel(tc, table, wq, wk, offs, out):
 
         zeros = held.tile([P, BANK], BF16, name="zeros")
         nc.vector.memset(zeros[:], 0.0)
-        warm_ps = psum.tile([P, BANK], F32, name="warm_ps", tag="left")
+        warm_ps = psum.tile([P, BANK], F32, name="warm_ps", tag="vector")
         for _ in range(WARM_UP):
             nc.tensor.matmul(warm_ps[:], zeros[:, 0:P], zeros[:], start=True, stop=True)
 
-        q_left = held.tile([D, HALF], BF16, name="q_left")
-        q_right = held.tile([D, HALF], BF16, name="q_right")
+        def psum_tile(i, shape, dtype):
+            return psum.tile(shape, dtype, name="ps_scalar" if i % 2 else "ps_vector", tag="scalar" if i % 2 else "vector")
+
+        def copy_out(i, dst, src):
+            if i % 2:
+                nc.scalar.activation(dst, src, COPY)
+            else:
+                nc.vector.tensor_copy(dst, src)
+
+        def scale_out(i, dst, src, scale):
+            if i % 2:
+                nc.scalar.activation(dst, src, COPY, scale=scale)
+            else:
+                nc.vector.tensor_scalar_mul(dst, src, scale)
+
+        q_sb = held.tile([D, N], BF16, name="q_sb")
         k_sb = held.tile([D, S], BF16, name="k_sb")
 
         def project_keys(g):
             first, end = groups[g]
             steps = slice(first * P, end * P)
-            if g % 2 == 0:
-                k_ps = psum.tile([D, (end - first) * P], BF16, name="k_ps_right", tag="right")
-                nc.tensor.matmul(k_ps[:], wk_sb[:], table_sb[:, steps], start=True, stop=True)
-                nc.scalar.activation(k_sb[:, steps], k_ps[:], COPY)
-            else:
-                k_ps = psum.tile([D, (end - first) * P], BF16, name="k_ps_left", tag="left")
-                nc.tensor.matmul(k_ps[:], wk_sb[:], table_sb[:, steps], start=True, stop=True)
-                nc.vector.tensor_copy(k_sb[:, steps], k_ps[:])
+            k_ps = psum_tile(g, [D, (end - first) * P], BF16)
+            nc.tensor.matmul(k_ps[:], wk_sb[:], table_sb[:, steps], start=True, stop=True)
+            copy_out(g, k_sb[:, steps], k_ps[:])
 
-        q_ps_left = psum.tile([D, HALF], F32, name="q_ps_left", tag="left")
-        nc.tensor.matmul(
-            q_ps_left[:], wq_sb[:], table_sb[:].indirect(offsets[:, 0 : HALF // 16]), start=True, stop=True
-        )
-        nc.vector.tensor_copy(q_left[:], q_ps_left[:])
         project_keys(0)
-        q_ps_right = psum.tile([D, HALF], F32, name="q_ps_right", tag="right")
-        nc.tensor.matmul(
-            q_ps_right[:], wq_sb[:], table_sb[:].indirect(offsets[:, HALF // 16 : N // 16]), start=True, stop=True
-        )
-        nc.scalar.activation(q_right[:], q_ps_right[:], COPY)
+
+        for i in range(N // LOOK_UP):
+            picked = slice(i * LOOK_UP, (i + 1) * LOOK_UP)
+            q_ps = psum_tile(i, [D, LOOK_UP], F32)
+            nc.tensor.matmul(
+                q_ps[:],
+                wq_sb[:],
+                table_sb[:].indirect(offsets[:, i * LOOK_UP // 16 : (i + 1) * LOOK_UP // 16]),
+                start=True,
+                stop=True,
+            )
+            copy_out(i, q_sb[:, picked], q_ps[:])
 
         for g, (first, end) in enumerate(groups):
             if g + 1 < len(groups):
@@ -86,11 +97,11 @@ def tile_informermodel_kernel(tc, table, wq, wk, offs, out):
             steps = slice(first * P, end * P)
             k_blocks = k_sb[:, steps].rearrange("m (p r) -> m r p", r=width)
             scores = held.tile([P, width, N], F32, name=f"scores{g}")
+            piece = LOOK_UP if g == 0 else N // 2
             for r in range(width):
-                s_ps_left = psum.tile([P, HALF], F32, name="s_ps_left", tag="left")
-                nc.tensor.matmul(s_ps_left[:], k_blocks[:, r, :], q_left[:], start=True, stop=True)
-                nc.vector.tensor_scalar_mul(scores[:, r, 0:HALF], s_ps_left[:], inv_sqrt_d)
-                s_ps_right = psum.tile([P, HALF], F32, name="s_ps_right", tag="right")
-                nc.tensor.matmul(s_ps_right[:], k_blocks[:, r, :], q_right[:], start=True, stop=True)
-                nc.scalar.activation(scores[:, r, HALF:N], s_ps_right[:], COPY, scale=inv_sqrt_d)
+                for i in range(N // piece):
+                    queries = slice(i * piece, (i + 1) * piece)
+                    s_ps = psum_tile(i, [P, piece], F32)
+                    nc.tensor.matmul(s_ps[:], k_blocks[:, r, :], q_sb[:, queries], start=True, stop=True)
+                    scale_out(i, scores[:, r, queries], s_ps[:], inv_sqrt_d)
             nc.sync.dma_start(out[steps, :].rearrange("(p r) j -> p r j", r=width), scores[:])

@@ -19,10 +19,12 @@ FLOPS = 2 * D * D * N + 2 * D * D * S + 2 * D * S * N
 def doubling_groups(blocks):
     groups = []
     first = 0
+    width = 1
     while first < blocks:
-        width = max(first, 1)
-        groups.append((first, first + width))
-        first += width
+        end = min(first + width, blocks)
+        groups.append((first, end))
+        first = end
+        width *= 2
     return groups
 
 

@@ -7,7 +7,7 @@ S = 1024
 N = 512
 P = 128
 BANK = 512
-WARM_UP = 4
+WARM_UP = 16
 LOOK_UP = 128
 
 BF16, F32, U16 = mybir.dt.bfloat16, mybir.dt.float32, mybir.dt.uint16
@@ -16,7 +16,7 @@ COPY = mybir.ActivationFunctionType.Copy
 FLOPS = 2 * D * D * N + 2 * D * D * S + 2 * D * S * N
 
 
-def doubling_groups(blocks):
+def growing_groups(blocks):
     groups = []
     first = 0
     width = 1
@@ -24,7 +24,7 @@ def doubling_groups(blocks):
         end = min(first + width, blocks)
         groups.append((first, end))
         first = end
-        width *= 2
+        width += 1
     return groups
 
 
@@ -32,7 +32,7 @@ def tile_informermodel_kernel(tc, table, wq, wk, offs, out):
     nc = tc.nc
     inv_sqrt_d = 1.0 / math.sqrt(D)
 
-    groups = doubling_groups(S // P)
+    groups = growing_groups(S // P)
 
     with (
         tc.tile_pool(name="held", bufs=1) as held,
@@ -47,11 +47,11 @@ def tile_informermodel_kernel(tc, table, wq, wk, offs, out):
         wq_sb = held.tile([D, D], BF16, name="wq_sb")
         nc.sync.dma_start(wq_sb[:], wq)
 
-        zeros = held.tile([P, BANK], BF16, name="zeros")
+        zeros = held.tile([P, P], BF16, name="zeros")
         nc.vector.memset(zeros[:], 0.0)
-        warm_ps = psum.tile([P, BANK], F32, name="warm_ps", tag="vector")
+        warm_ps = psum.tile([P, P], F32, name="warm_ps", tag="vector")
         for _ in range(WARM_UP):
-            nc.tensor.matmul(warm_ps[:], zeros[:, 0:P], zeros[:], start=True, stop=True)
+            nc.tensor.matmul(warm_ps[:], zeros[:], zeros[:], start=True, stop=True)
 
         def psum_tile(i, shape, dtype):
             return psum.tile(shape, dtype, name="ps_scalar" if i % 2 else "ps_vector", tag="scalar" if i % 2 else "vector")

@@ -92,9 +92,11 @@ def tile_informermodel_kernel(tc, table, wq, wk, offs, out):
             )
             copy_out(i, q_sb[:, picked], q_ps[:])
 
+        project_keys(1)
+
         for g, (first, end) in enumerate(groups):
-            if g + 1 < len(groups):
-                project_keys(g + 1)
+            if g + 2 < len(groups):
+                project_keys(g + 2)
             width = end - first
             steps = slice(first * P, end * P)
             k_blocks = k_sb[:, steps].rearrange("m (p r) -> m r p", r=width)

@@ -41,11 +41,11 @@ def tile_informermodel_kernel(tc, table, wq, wk, offs, out):
         table_sb = held.tile([D, S], BF16, name="table_sb")
         nc.sync.dma_start(table_sb[:], table)
         wk_sb = held.tile([D, D], BF16, name="wk_sb")
-        nc.sync.dma_start(wk_sb[:], wk)
+        nc.scalar.dma_start(wk_sb[:], wk)
         offsets = held.tile([P, N // 16], U16, name="offsets")
         nc.sync.dma_start(offsets[:], offs)
         wq_sb = held.tile([D, D], BF16, name="wq_sb")
-        nc.sync.dma_start(wq_sb[:], wq)
+        nc.scalar.dma_start(wq_sb[:], wq)
 
         zeros = held.tile([P, P], BF16, name="zeros")
         nc.vector.memset(zeros[:], 0.0)

@@ -62,6 +62,12 @@ def tile_informermodel_kernel(tc, table, wq, wk, offs, out):
             else:
                 nc.vector.tensor_copy(dst, src)
 
+        def copy_bf16_out(i, dst, src):
+            if i % 2:
+                nc.scalar.copy(dst, src)
+            else:
+                nc.vector.tensor_copy(dst, src)
+
         def scale_out(i, dst, src, scale):
             if i % 2:
                 nc.scalar.activation(dst, src, COPY, scale=scale)
@@ -76,7 +82,7 @@ def tile_informermodel_kernel(tc, table, wq, wk, offs, out):
             steps = slice(first * P, end * P)
             k_ps = psum_tile(g, [D, (end - first) * P], BF16)
             nc.tensor.matmul(k_ps[:], wk_sb[:], table_sb[:, steps], start=True, stop=True)
-            copy_out(g, k_sb[:, steps], k_ps[:])
+            copy_bf16_out(g, k_sb[:, steps], k_ps[:])
 
         project_keys(0)
 
@@ -93,10 +99,11 @@ def tile_informermodel_kernel(tc, table, wq, wk, offs, out):
             copy_out(i, q_sb[:, picked], q_ps[:])
 
         project_keys(1)
+        project_keys(2)
 
         for g, (first, end) in enumerate(groups):
-            if g + 2 < len(groups):
-                project_keys(g + 2)
+            if g == 2:
+                project_keys(3)
             width = end - first
             steps = slice(first * P, end * P)
             k_blocks = k_sb[:, steps].rearrange("m (p r) -> m r p", r=width)

@@ -107,7 +107,7 @@ def tile_informermodel_kernel(tc, table, wq, wk, offs, out):
             width = end - first
             steps = slice(first * P, end * P)
             k_blocks = k_sb[:, steps].rearrange("m (p r) -> m r p", r=width)
-            scores = held.tile([P, width, N], F32, name=f"scores{g}")
+            scores = held.tile([P, width, N], F32, name=f"scores{g}", align_bytes=256)
             piece = LOOK_UP if g == 0 else N // 2
             for r in range(width):
                 for i in range(N // piece):

@@ -44,7 +44,7 @@ def tile_informermodel_kernel(tc, table, wq, wk, offs, out):
         nc.scalar.dma_start(wk_sb[:], wk)
         offsets = held.tile([P, N // 16], U16, name="offsets")
         nc.sync.dma_start(offsets[:], offs)
-        wq_sb = held.tile([D, D], BF16, name="wq_sb")
+        wq_sb = held.tile([D, D], BF16, name="wq_sb", align_bytes=256)
         nc.scalar.dma_start(wq_sb[:], wq)
 
         zeros = held.tile([P, P], BF16, name="zeros")

@@ -16,15 +16,12 @@ COPY = mybir.ActivationFunctionType.Copy
 FLOPS = 2 * D * D * N + 2 * D * D * S + 2 * D * S * N
 
 
-def growing_groups(blocks):
+def runs(widths):
     groups = []
     first = 0
-    width = 1
-    while first < blocks:
-        end = min(first + width, blocks)
-        groups.append((first, end))
-        first = end
-        width += 1
+    for width in widths:
+        groups.append((first, first + width))
+        first += width
     return groups
 
 
@@ -32,7 +29,7 @@ def tile_informermodel_kernel(tc, table, wq, wk, offs, out):
     nc = tc.nc
     inv_sqrt_d = 1.0 / math.sqrt(D)
 
-    groups = growing_groups(S // P)
+    groups = runs([1, 2, 2, 3])
 
     with (
         tc.tile_pool(name="held", bufs=1) as held,

import math

import concourse.mybir as mybir

D = 128
S = 1024
N = 512
P = 128
BANK = 512
WARM_UP = 16
LOOK_UP = 128

BF16, F32, U16 = mybir.dt.bfloat16, mybir.dt.float32, mybir.dt.uint16
COPY = mybir.ActivationFunctionType.Copy

FLOPS = 2 * D * D * N + 2 * D * D * S + 2 * D * S * N


def runs(widths):
    groups = []
    first = 0
    for width in widths:
        groups.append((first, first + width))
        first += width
    return groups


def tile_informermodel_kernel(tc, table, wq, wk, offs, out):
    nc = tc.nc
    inv_sqrt_d = 1.0 / math.sqrt(D)

    groups = runs([1, 2, 2, 3])

    with (
        tc.tile_pool(name="held", bufs=1) as held,
        tc.psum_pool(name="psum", bufs=4) as psum,
    ):
        table_sb = held.tile([D, S], BF16, name="table_sb")
        nc.sync.dma_start(table_sb[:], table)
        wk_sb = held.tile([D, D], BF16, name="wk_sb")
        nc.scalar.dma_start(wk_sb[:], wk)
        offsets = held.tile([P, N // 16], U16, name="offsets")
        nc.sync.dma_start(offsets[:], offs)
        wq_sb = held.tile([D, D], BF16, name="wq_sb", align_bytes=256)
        nc.scalar.dma_start(wq_sb[:], wq)

        zeros = held.tile([P, P], BF16, name="zeros")
        nc.vector.memset(zeros[:], 0.0)
        warm_ps = psum.tile([P, P], F32, name="warm_ps", tag="vector")
        for _ in range(WARM_UP):
            nc.tensor.matmul(warm_ps[:], zeros[:], zeros[:], start=True, stop=True)

        def psum_tile(i, shape, dtype):
            return psum.tile(shape, dtype, name="ps_scalar" if i % 2 else "ps_vector", tag="scalar" if i % 2 else "vector")

        def copy_out(i, dst, src):
            if i % 2:
                nc.scalar.activation(dst, src, COPY)
            else:
                nc.vector.tensor_copy(dst, src)

        def copy_bf16_out(i, dst, src):
            if i % 2:
                nc.scalar.copy(dst, src)
            else:
                nc.vector.tensor_copy(dst, src)

        def scale_out(i, dst, src, scale):
            if i % 2:
                nc.scalar.activation(dst, src, COPY, scale=scale)
            else:
                nc.vector.tensor_scalar_mul(dst, src, scale)

        q_sb = held.tile([D, N], BF16, name="q_sb")
        k_sb = held.tile([D, S], BF16, name="k_sb")

        def project_keys(g):
            first, end = groups[g]
            steps = slice(first * P, end * P)
            k_ps = psum_tile(g, [D, (end - first) * P], BF16)
            nc.tensor.matmul(k_ps[:], wk_sb[:], table_sb[:, steps], start=True, stop=True)
            copy_bf16_out(g, k_sb[:, steps], k_ps[:])

        project_keys(0)

        for i in range(N // LOOK_UP):
            picked = slice(i * LOOK_UP, (i + 1) * LOOK_UP)
            q_ps = psum_tile(i, [D, LOOK_UP], F32)
            nc.tensor.matmul(
                q_ps[:],
                wq_sb[:],
                table_sb[:].indirect(offsets[:, i * LOOK_UP // 16 : (i + 1) * LOOK_UP // 16]),
                start=True,
                stop=True,
            )
            copy_out(i, q_sb[:, picked], q_ps[:])

        project_keys(1)
        project_keys(2)

        for g, (first, end) in enumerate(groups):
            if g == 2:
                project_keys(3)
            width = end - first
            steps = slice(first * P, end * P)
            k_blocks = k_sb[:, steps].rearrange("m (p r) -> m r p", r=width)
            scores = held.tile([P, width, N], F32, name=f"scores{g}", align_bytes=256)
            piece = LOOK_UP if g == 0 else N // 2
            for r in range(width):
                for i in range(N // piece):
                    queries = slice(i * piece, (i + 1) * piece)
                    s_ps = psum_tile(i, [P, piece], F32)
                    nc.tensor.matmul(s_ps[:], k_blocks[:, r, :], q_sb[:, queries], start=True, stop=True)
                    scale_out(i, scores[:, r, queries], s_ps[:], inv_sqrt_d)
            nc.sync.dma_start(out[steps, :].rearrange("(p r) j -> p r j", r=width), scores[:])
